import numpy as np
import ml_dtypes


def mxq(x, axis, fmt="e4m3"):
    dtype, down = {"e4m3": (ml_dtypes.float8_e4m3fn, 7), "e5m2": (ml_dtypes.float8_e5m2, 14)}[fmt]
    v = np.moveaxis(np.asarray(x, np.float32).astype(ml_dtypes.bfloat16).astype(np.float64), axis, -1)
    blocks = v.reshape(v.shape[:-1] + (-1, 32))
    amax = np.abs(blocks).max(-1, keepdims=True)
    byte = np.maximum(np.where(amax > 0, np.frexp(amax)[1] - 1 + 127, 0) - down, 1)
    scale = np.exp2(byte - 127.0)
    codes = (blocks / scale).astype(np.float32).astype(dtype).astype(np.float64)
    return np.moveaxis((codes * scale).reshape(v.shape), -1, axis)


WIDE = False


def mx_kscale(k):
    if not WIDE:
        return np.ones(k)
    levels = np.array([10, -10, 5, -5, 0])
    a = np.random.permutation(np.resize(levels, k // 512 * 4)).reshape(k // 512, 4)
    idx = np.arange(k)
    return np.exp2(a[idx // 512, idx % 128 // 32])


BF16 = ml_dtypes.bfloat16


def bf(x):
    return np.asarray(x, np.float32).astype(BF16)


def f64(x):
    return np.asarray(x).astype(np.float64)


N, H, O, L = 1024, 512, 512, 4


def represent(h):
    n = h.shape[0]
    total = np.sum(h, axis=0, keepdims=True)
    return (n * h - total) / (n - 1)


def sigmoid(v):
    return 1.0 / (1.0 + np.exp(-v))


def setup_inputs():
    t = mx_kscale(H)
    mu = np.random.standard_normal(H)
    return {"h": bf((np.random.standard_normal((N, H)) * 1.2 + mu) * t),
            "w": bf(np.random.standard_normal((H, H)) * 0.6 / np.sqrt(H) * t[:, None] / t[None, :]),
            "w_ff": bf(np.random.standard_normal((O, H)) * 0.6 / np.sqrt(H) / t[None, :]),
            "b_ff": bf(np.random.standard_normal(O) * 0.3)}


def reference(h, w, w_ff, b_ff):
    h = f64(h)
    r = represent(h)
    f = mxq(r, 1, "e4m3") @ mxq(f64(w), 1, "e4m3").T
    h_new = f + h
    return sigmoid((mxq(h_new, 1, "e4m3") @ mxq(f64(w_ff), 1, "e4m3").T) + f64(b_ff))

@@ -1,0 +1,209 @@
+from contextlib import ExitStack
+
+import concourse.mybir as mybir
+from concourse.masks import make_identity
+
+F32 = mybir.dt.float32
+BF16 = mybir.dt.bfloat16
+U32 = mybir.dt.uint32
+U8 = mybir.dt.uint8
+FP8X4 = mybir.dt.float8_e4m3fn_x4
+ALU = mybir.AluOpType
+ACT = mybir.ActivationFunctionType
+
+P = 128
+PACK = 4
+ITEMS = 1024
+HID = 512
+OUT = 512
+ITEM_TILES = ITEMS // P
+HID_TILES = HID // P
+PAIR = 2 * P
+HALF = ITEMS // 2
+SUM_COLS = 32
+
+FLOPS = 2 * ITEMS * HID * HID + 2 * ITEMS * HID * OUT
+
+
+def tile_differ_amplifier_pa_kernel(tc, h, w, w_ff, b_ff, out):
+    nc = tc.nc
+    with ExitStack() as ctx:
+        keep = ctx.enter_context(tc.tile_pool(name="keep", bufs=1))
+        stream = ctx.enter_context(tc.tile_pool(name="stream", bufs=4))
+        banks = ctx.enter_context(tc.psum_pool(name="banks", bufs=7))
+        sum_bank = ctx.enter_context(tc.psum_pool(name="sum_bank", bufs=1))
+
+        h_sb = keep.tile([P, ITEM_TILES * HID], BF16)
+        h_rows = h.rearrange("(p a) k -> p (a k)", a=ITEM_TILES)
+        for c in range(ITEM_TILES // 2):
+            cols = slice(c * 2 * HID, (c + 1) * 2 * HID)
+            nc.sync.dma_start(out=h_sb[:, cols], in_=h_rows[:, cols])
+        w_sb = keep.tile([P, HID_TILES * HID], BF16)
+        nc.sync.dma_start(
+            out=w_sb[:].rearrange("p (u x) -> p u x", u=2),
+            in_=w.rearrange("(u p e) k -> p u (e k)", u=2, e=2),
+        )
+        wf_sb = keep.tile([P, HID_TILES * HID], BF16)
+        nc.sync.dma_start(
+            out=wf_sb[:].rearrange("p (t k) -> p t k", t=HID_TILES),
+            in_=w_ff.rearrange("(t p) k -> p t k", p=P),
+        )
+        bias = keep.tile([P, OUT], BF16)
+        nc.sync.dma_start(out=bias[:], in_=b_ff.partition_broadcast(P))
+
+        ident = keep.tile([P, P], F32)
+        make_identity(nc, ident[:])
+        pick = keep.tile([P, PACK, SUM_COLS], BF16)
+        nc.vector.memset(pick[:], 0.0)
+        for t in range(PACK):
+            nc.vector.memset(pick[:, t, 8 * t : 8 * t + 8], 1.0)
+        warm = keep.tile([P, 1], F32)
+        nc.vector.memset(warm[:], 0.0)
+        nc.scalar.activation(out=warm[:], in_=warm[:], func=ACT.Sigmoid)
+
+        def transpose_pair(rows_words, grouped_words):
+            bank = banks.tile([P, 2, PAIR], F32, tag="bank")
+            for i in range(2):
+                for u in range(2):
+                    nc.tensor.transpose(
+                        bank[:, u, i * P : (i + 1) * P], rows_words[:, i, u * P : (u + 1) * P], ident[:]
+                    )
+            nc.scalar.copy(out=grouped_words, in_=bank[:].rearrange("p u c -> p c u"))
+
+        def quantise(grouped, codes, scales, first, count):
+            nc.vector.quantize_mx(
+                out=codes[:, first : first + count].bitcast(FP8X4),
+                scales=scales[:, first : first + count],
+                in_=grouped[:, PACK * first : PACK * (first + count)],
+            )
+
+        def words_by_tile(rows, tiles):
+            return rows[:].bitcast(F32).rearrange("p (a q) -> p a q", a=tiles)
+
+        def words_by_column(grouped):
+            return grouped[:].bitcast(F32).rearrange("p (c u) -> p c u", u=2)
+
+        def by_column(grouped):
+            return grouped[:].rearrange("p (c t) -> p c t", t=PACK)
+
+        h_by_value = h_sb[:].rearrange("p (a u q e) -> p a u q e", a=ITEM_TILES, u=2, e=2)
+        total = sum_bank.tile([P, SUM_COLS], F32)
+
+        def column_sums(c):
+            for a in (2 * c, 2 * c + 1):
+                for t in range(PACK):
+                    nc.tensor.matmul(
+                        out=total[:],
+                        lhsT=h_by_value[:, a, t // 2, :, t % 2],
+                        rhs=pick[:, t, :],
+                        start=(a == 0 and t == 0),
+                        stop=(a == ITEM_TILES - 1 and t == PACK - 1),
+                    )
+
+        h_grouped = keep.tile([P, ITEMS * PACK], BF16, align_bytes=64)
+
+        def transpose_h(c):
+            transpose_pair(
+                words_by_tile(h_sb, ITEM_TILES)[:, 2 * c : 2 * c + 2, :],
+                words_by_column(h_grouped)[:, c * PAIR : (c + 1) * PAIR, :],
+            )
+
+        column_sums(0)
+        transpose_h(0)
+        for c in range(1, ITEM_TILES // 2):
+            column_sums(c)
+        for c in range(1, ITEM_TILES // 2):
+            transpose_h(c)
+
+        w_grouped = keep.tile([P, HID * PACK], BF16, align_bytes=64)
+        wf_grouped = keep.tile([P, OUT * PACK], BF16, align_bytes=64)
+        for rows, grouped in ((w_sb, w_grouped), (wf_sb, wf_grouped)):
+            for c in range(HID_TILES // 2):
+                transpose_pair(
+                    words_by_tile(rows, HID_TILES)[:, 2 * c : 2 * c + 2, :],
+                    words_by_column(grouped)[:, c * PAIR : (c + 1) * PAIR, :],
+                )
+        w_codes = keep.tile([P, HID], U32, align_bytes=64)
+        w_scales = keep.tile([P, HID], U8, align_bytes=64)
+        wf_codes = keep.tile([P, OUT], U32, align_bytes=64)
+        wf_scales = keep.tile([P, OUT], U8, align_bytes=64)
+
+        shift = keep.tile([P, PACK], F32)
+        nc.vector.tensor_scalar_mul(
+            out=shift[:],
+            in0=total[:].rearrange("p (t c) -> p t c", t=PACK)[:, :, 0],
+            scalar1=1.0 / (ITEMS - 1),
+        )
+        r_grouped = keep.tile([P, ITEMS * PACK], BF16, align_bytes=64)
+        r_codes = keep.tile([P, ITEMS], U32, align_bytes=64)
+        r_scales = keep.tile([P, ITEMS], U8, align_bytes=64)
+
+        def centre(c):
+            cols = slice(c * PAIR, (c + 1) * PAIR)
+            nc.vector.scalar_tensor_tensor(
+                out=by_column(r_grouped)[:, cols, :],
+                in0=by_column(h_grouped)[:, cols, :],
+                scalar=ITEMS / (ITEMS - 1),
+                in1=shift[:].unsqueeze(1).to_broadcast([P, PAIR, PACK]),
+                op0=ALU.mult,
+                op1=ALU.subtract,
+            )
+
+        centre(0)
+        centre(1)
+        quantise(r_grouped, r_codes, r_scales, 0, HALF)
+        centre(2)
+        centre(3)
+        quantise(w_grouped, w_codes, w_scales, 0, HID)
+        quantise(r_grouped, r_codes, r_scales, HALF, HALF)
+
+        n_grouped = keep.tile([P, ITEMS * PACK], BF16, align_bytes=64)
+        n_codes = keep.tile([P, ITEMS], U32, align_bytes=64)
+        n_scales = keep.tile([P, ITEMS], U8, align_bytes=64)
+
+        def first_product(a):
+            items = slice(a * P, (a + 1) * P)
+            product = banks.tile([P, PACK, P], F32, tag="bank")
+            for t in range(PACK):
+                units = slice(t * P, (t + 1) * P)
+                nc.tensor.matmul_mx(
+                    out=product[:, t, :],
+                    lhsT=w_codes[:, units].bitcast(FP8X4),
+                    lhsT_scale=w_scales[:, units],
+                    rhs=r_codes[:, items].bitcast(FP8X4),
+                    rhs_scale=r_scales[:, items],
+                    start=True,
+                    stop=True,
+                )
+            nc.vector.tensor_tensor(
+                out=by_column(n_grouped)[:, items, :],
+                in0=product[:].rearrange("p t n -> p n t"),
+                in1=by_column(h_grouped)[:, items, :],
+                op=ALU.add,
+            )
+
+        for a in range(ITEM_TILES // 2):
+            first_product(a)
+        quantise(wf_grouped, wf_codes, wf_scales, 0, OUT)
+        quantise(n_grouped, n_codes, n_scales, 0, HALF)
+        for a in range(ITEM_TILES // 2, ITEM_TILES):
+            first_product(a)
+        quantise(n_grouped, n_codes, n_scales, HALF, HALF)
+
+        out_rows = out.rearrange("(p a) o -> p a o", a=ITEM_TILES)
+        for a in range(ITEM_TILES):
+            items = slice(a * P, (a + 1) * P)
+            product = banks.tile([P, OUT], F32, tag="bank")
+            nc.tensor.matmul_mx(
+                out=product[:],
+                lhsT=n_codes[:, items].bitcast(FP8X4),
+                lhsT_scale=n_scales[:, items],
+                rhs=wf_codes[:].bitcast(FP8X4),
+                rhs_scale=wf_scales[:],
+                start=True,
+                stop=True,
+            )
+            result = stream.tile([P, OUT], F32)
+            nc.vector.tensor_tensor(out=result[:], in0=product[:], in1=bias[:], op=ALU.add)
+            nc.scalar.activation(out=result[:], in_=result[:], func=ACT.Sigmoid)
+            nc.sync.dma_start(out=out_rows[:, a, :], in_=result[:])

@@ -32,6 +32,7 @@ def tile_differ_amplifier_pa_kernel(tc, h, w, w_ff, b_ff, out):
         stream = ctx.enter_context(tc.tile_pool(name="stream", bufs=4))
         banks = ctx.enter_context(tc.psum_pool(name="banks", bufs=7))
         sum_bank = ctx.enter_context(tc.psum_pool(name="sum_bank", bufs=1))
+        ctx.enter_context(tc.manual_schedule())
 
         h_sb = keep.tile([P, ITEM_TILES * HID], BF16)
         h_rows = h.rearrange("(p a) k -> p (a k)", a=ITEM_TILES)
@@ -151,8 +152,8 @@ def tile_differ_amplifier_pa_kernel(tc, h, w, w_ff, b_ff, out):
 
         centre(0)
         centre(1)
-        quantise(r_grouped, r_codes, r_scales, 0, HALF)
         centre(2)
+        quantise(r_grouped, r_codes, r_scales, 0, HALF)
         centre(3)
         quantise(w_grouped, w_codes, w_scales, 0, HID)
         quantise(r_grouped, r_codes, r_scales, HALF, HALF)

@@ -21,6 +21,8 @@ HID_TILES = HID // P
 PAIR = 2 * P
 HALF = ITEMS // 2
 SUM_COLS = 32
+QUANTISE_LAG = 1
+SECOND_LAG = 3
 
 FLOPS = 2 * ITEMS * HID * HID + 2 * ITEMS * HID * OUT
 
@@ -29,7 +31,7 @@ def tile_differ_amplifier_pa_kernel(tc, h, w, w_ff, b_ff, out):
     nc = tc.nc
     with ExitStack() as ctx:
         keep = ctx.enter_context(tc.tile_pool(name="keep", bufs=1))
-        stream = ctx.enter_context(tc.tile_pool(name="stream", bufs=4))
+        results = ctx.enter_context(tc.tile_pool(name="results", bufs=ITEM_TILES))
         banks = ctx.enter_context(tc.psum_pool(name="banks", bufs=7))
         sum_bank = ctx.enter_context(tc.psum_pool(name="sum_bank", bufs=1))
         ctx.enter_context(tc.manual_schedule())
@@ -183,16 +185,9 @@ def tile_differ_amplifier_pa_kernel(tc, h, w, w_ff, b_ff, out):
                 op=ALU.add,
             )
 
-        for a in range(ITEM_TILES // 2):
-            first_product(a)
-        quantise(wf_grouped, wf_codes, wf_scales, 0, OUT)
-        quantise(n_grouped, n_codes, n_scales, 0, HALF)
-        for a in range(ITEM_TILES // 2, ITEM_TILES):
-            first_product(a)
-        quantise(n_grouped, n_codes, n_scales, HALF, HALF)
-
         out_rows = out.rearrange("(p a) o -> p a o", a=ITEM_TILES)
-        for a in range(ITEM_TILES):
+
+        def second_product(a):
             items = slice(a * P, (a + 1) * P)
             product = banks.tile([P, OUT], F32, tag="bank")
             nc.tensor.matmul_mx(
@@ -204,7 +199,16 @@ def tile_differ_amplifier_pa_kernel(tc, h, w, w_ff, b_ff, out):
                 start=True,
                 stop=True,
             )
-            result = stream.tile([P, OUT], F32)
+            result = results.tile([P, OUT], F32)
             nc.vector.tensor_tensor(out=result[:], in0=product[:], in1=bias[:], op=ALU.add)
             nc.scalar.activation(out=result[:], in_=result[:], func=ACT.Sigmoid)
             nc.sync.dma_start(out=out_rows[:, a, :], in_=result[:])
+
+        quantise(wf_grouped, wf_codes, wf_scales, 0, OUT)
+        for step in range(ITEM_TILES + SECOND_LAG):
+            if step < ITEM_TILES:
+                first_product(step)
+            if 0 <= step - QUANTISE_LAG < ITEM_TILES:
+                quantise(n_grouped, n_codes, n_scales, (step - QUANTISE_LAG) * P, P)
+            if 0 <= step - SECOND_LAG:
+                second_product(step - SECOND_LAG)

@@ -23,6 +23,7 @@ HALF = ITEMS // 2
 SUM_COLS = 32
 QUANTISE_LAG = 1
 SECOND_LAG = 3
+FINISH_LAG = 5
 
 FLOPS = 2 * ITEMS * HID * HID + 2 * ITEMS * HID * OUT
 
@@ -199,16 +200,26 @@ def tile_differ_amplifier_pa_kernel(tc, h, w, w_ff, b_ff, out):
                 start=True,
                 stop=True,
             )
-            result = results.tile([P, OUT], F32)
-            nc.vector.tensor_tensor(out=result[:], in0=product[:], in1=bias[:], op=ALU.add)
+            result = results.tile([P, OUT], F32, name="result")
+            if a % 2 == 0 and a < ITEM_TILES - 2:
+                nc.scalar.copy(out=result[:], in_=product[:])
+                nc.gpsimd.tensor_tensor(out=result[:], in0=result[:], in1=bias[:], op=ALU.add)
+            else:
+                nc.vector.tensor_tensor(out=result[:], in0=product[:], in1=bias[:], op=ALU.add)
+            return result
+
+        def finish(a, result):
             nc.scalar.activation(out=result[:], in_=result[:], func=ACT.Sigmoid)
             nc.sync.dma_start(out=out_rows[:, a, :], in_=result[:])
 
         quantise(wf_grouped, wf_codes, wf_scales, 0, OUT)
-        for step in range(ITEM_TILES + SECOND_LAG):
+        biased = []
+        for step in range(ITEM_TILES + FINISH_LAG):
             if step < ITEM_TILES:
                 first_product(step)
             if 0 <= step - QUANTISE_LAG < ITEM_TILES:
                 quantise(n_grouped, n_codes, n_scales, (step - QUANTISE_LAG) * P, P)
-            if 0 <= step - SECOND_LAG:
-                second_product(step - SECOND_LAG)
+            if 0 <= step - SECOND_LAG < ITEM_TILES:
+                biased.append(second_product(step - SECOND_LAG))
+            if 0 <= step - FINISH_LAG:
+                finish(step - FINISH_LAG, biased[step - FINISH_LAG])

from contextlib import ExitStack

import concourse.mybir as mybir
from concourse.masks import make_identity

F32 = mybir.dt.float32
BF16 = mybir.dt.bfloat16
U32 = mybir.dt.uint32
U8 = mybir.dt.uint8
FP8X4 = mybir.dt.float8_e4m3fn_x4
ALU = mybir.AluOpType
ACT = mybir.ActivationFunctionType

P = 128
PACK = 4
ITEMS = 1024
HID = 512
OUT = 512
ITEM_TILES = ITEMS // P
HID_TILES = HID // P
PAIR = 2 * P
HALF = ITEMS // 2
SUM_COLS = 32
QUANTISE_LAG = 1
SECOND_LAG = 3
FINISH_LAG = 5

FLOPS = 2 * ITEMS * HID * HID + 2 * ITEMS * HID * OUT


def tile_differ_amplifier_pa_kernel(tc, h, w, w_ff, b_ff, out):
    nc = tc.nc
    with ExitStack() as ctx:
        keep = ctx.enter_context(tc.tile_pool(name="keep", bufs=1))
        results = ctx.enter_context(tc.tile_pool(name="results", bufs=ITEM_TILES))
        banks = ctx.enter_context(tc.psum_pool(name="banks", bufs=7))
        sum_bank = ctx.enter_context(tc.psum_pool(name="sum_bank", bufs=1))
        ctx.enter_context(tc.manual_schedule())

        h_sb = keep.tile([P, ITEM_TILES * HID], BF16)
        h_rows = h.rearrange("(p a) k -> p (a k)", a=ITEM_TILES)
        for c in range(ITEM_TILES // 2):
            cols = slice(c * 2 * HID, (c + 1) * 2 * HID)
            nc.sync.dma_start(out=h_sb[:, cols], in_=h_rows[:, cols])
        w_sb = keep.tile([P, HID_TILES * HID], BF16)
        nc.sync.dma_start(
            out=w_sb[:].rearrange("p (u x) -> p u x", u=2),
            in_=w.rearrange("(u p e) k -> p u (e k)", u=2, e=2),
        )
        wf_sb = keep.tile([P, HID_TILES * HID], BF16)
        nc.sync.dma_start(
            out=wf_sb[:].rearrange("p (t k) -> p t k", t=HID_TILES),
            in_=w_ff.rearrange("(t p) k -> p t k", p=P),
        )
        bias = keep.tile([P, OUT], BF16)
        nc.sync.dma_start(out=bias[:], in_=b_ff.partition_broadcast(P))

        ident = keep.tile([P, P], F32)
        make_identity(nc, ident[:])
        pick = keep.tile([P, PACK, SUM_COLS], BF16)
        nc.vector.memset(pick[:], 0.0)
        for t in range(PACK):
            nc.vector.memset(pick[:, t, 8 * t : 8 * t + 8], 1.0)
        warm = keep.tile([P, 1], F32)
        nc.vector.memset(warm[:], 0.0)
        nc.scalar.activation(out=warm[:], in_=warm[:], func=ACT.Sigmoid)

        def transpose_pair(rows_words, grouped_words):
            bank = banks.tile([P, 2, PAIR], F32, tag="bank")
            for i in range(2):
                for u in range(2):
                    nc.tensor.transpose(
                        bank[:, u, i * P : (i + 1) * P], rows_words[:, i, u * P : (u + 1) * P], ident[:]
                    )
            nc.scalar.copy(out=grouped_words, in_=bank[:].rearrange("p u c -> p c u"))

        def quantise(grouped, codes, scales, first, count):
            nc.vector.quantize_mx(
                out=codes[:, first : first + count].bitcast(FP8X4),
                scales=scales[:, first : first + count],
                in_=grouped[:, PACK * first : PACK * (first + count)],
            )

        def words_by_tile(rows, tiles):
            return rows[:].bitcast(F32).rearrange("p (a q) -> p a q", a=tiles)

        def words_by_column(grouped):
            return grouped[:].bitcast(F32).rearrange("p (c u) -> p c u", u=2)

        def by_column(grouped):
            return grouped[:].rearrange("p (c t) -> p c t", t=PACK)

        h_by_value = h_sb[:].rearrange("p (a u q e) -> p a u q e", a=ITEM_TILES, u=2, e=2)
        total = sum_bank.tile([P, SUM_COLS], F32)

        def column_sums(c):
            for a in (2 * c, 2 * c + 1):
                for t in range(PACK):
                    nc.tensor.matmul(
                        out=total[:],
                        lhsT=h_by_value[:, a, t // 2, :, t % 2],
                        rhs=pick[:, t, :],
                        start=(a == 0 and t == 0),
                        stop=(a == ITEM_TILES - 1 and t == PACK - 1),
                    )

        h_grouped = keep.tile([P, ITEMS * PACK], BF16, align_bytes=64)

        def transpose_h(c):
            transpose_pair(
                words_by_tile(h_sb, ITEM_TILES)[:, 2 * c : 2 * c + 2, :],
                words_by_column(h_grouped)[:, c * PAIR : (c + 1) * PAIR, :],
            )

        column_sums(0)
        transpose_h(0)
        for c in range(1, ITEM_TILES // 2):
            column_sums(c)
        for c in range(1, ITEM_TILES // 2):
            transpose_h(c)

        w_grouped = keep.tile([P, HID * PACK], BF16, align_bytes=64)
        wf_grouped = keep.tile([P, OUT * PACK], BF16, align_bytes=64)
        for rows, grouped in ((w_sb, w_grouped), (wf_sb, wf_grouped)):
            for c in range(HID_TILES // 2):
                transpose_pair(
                    words_by_tile(rows, HID_TILES)[:, 2 * c : 2 * c + 2, :],
                    words_by_column(grouped)[:, c * PAIR : (c + 1) * PAIR, :],
                )
        w_codes = keep.tile([P, HID], U32, align_bytes=64)
        w_scales = keep.tile([P, HID], U8, align_bytes=64)
        wf_codes = keep.tile([P, OUT], U32, align_bytes=64)
        wf_scales = keep.tile([P, OUT], U8, align_bytes=64)

        shift = keep.tile([P, PACK], F32)
        nc.vector.tensor_scalar_mul(
            out=shift[:],
            in0=total[:].rearrange("p (t c) -> p t c", t=PACK)[:, :, 0],
            scalar1=1.0 / (ITEMS - 1),
        )
        r_grouped = keep.tile([P, ITEMS * PACK], BF16, align_bytes=64)
        r_codes = keep.tile([P, ITEMS], U32, align_bytes=64)
        r_scales = keep.tile([P, ITEMS], U8, align_bytes=64)

        def centre(c):
            cols = slice(c * PAIR, (c + 1) * PAIR)
            nc.vector.scalar_tensor_tensor(
                out=by_column(r_grouped)[:, cols, :],
                in0=by_column(h_grouped)[:, cols, :],
                scalar=ITEMS / (ITEMS - 1),
                in1=shift[:].unsqueeze(1).to_broadcast([P, PAIR, PACK]),
                op0=ALU.mult,
                op1=ALU.subtract,
            )

        centre(0)
        centre(1)
        centre(2)
        quantise(r_grouped, r_codes, r_scales, 0, HALF)
        centre(3)
        quantise(w_grouped, w_codes, w_scales, 0, HID)
        quantise(r_grouped, r_codes, r_scales, HALF, HALF)

        n_grouped = keep.tile([P, ITEMS * PACK], BF16, align_bytes=64)
        n_codes = keep.tile([P, ITEMS], U32, align_bytes=64)
        n_scales = keep.tile([P, ITEMS], U8, align_bytes=64)

        def first_product(a):
            items = slice(a * P, (a + 1) * P)
            product = banks.tile([P, PACK, P], F32, tag="bank")
            for t in range(PACK):
                units = slice(t * P, (t + 1) * P)
                nc.tensor.matmul_mx(
                    out=product[:, t, :],
                    lhsT=w_codes[:, units].bitcast(FP8X4),
                    lhsT_scale=w_scales[:, units],
                    rhs=r_codes[:, items].bitcast(FP8X4),
                    rhs_scale=r_scales[:, items],
                    start=True,
                    stop=True,
                )
            nc.vector.tensor_tensor(
                out=by_column(n_grouped)[:, items, :],
                in0=product[:].rearrange("p t n -> p n t"),
                in1=by_column(h_grouped)[:, items, :],
                op=ALU.add,
            )

        out_rows = out.rearrange("(p a) o -> p a o", a=ITEM_TILES)

        def second_product(a):
            items = slice(a * P, (a + 1) * P)
            product = banks.tile([P, OUT], F32, tag="bank")
            nc.tensor.matmul_mx(
                out=product[:],
                lhsT=n_codes[:, items].bitcast(FP8X4),
                lhsT_scale=n_scales[:, items],
                rhs=wf_codes[:].bitcast(FP8X4),
                rhs_scale=wf_scales[:],
                start=True,
                stop=True,
            )
            result = results.tile([P, OUT], F32, name="result")
            if a % 2 == 0 and a < ITEM_TILES - 2:
                nc.scalar.copy(out=result[:], in_=product[:])
                nc.gpsimd.tensor_tensor(out=result[:], in0=result[:], in1=bias[:], op=ALU.add)
            else:
                nc.vector.tensor_tensor(out=result[:], in0=product[:], in1=bias[:], op=ALU.add)
            return result

        def finish(a, result):
            nc.scalar.activation(out=result[:], in_=result[:], func=ACT.Sigmoid)
            nc.sync.dma_start(out=out_rows[:, a, :], in_=result[:])

        quantise(wf_grouped, wf_codes, wf_scales, 0, OUT)
        biased = []
        for step in range(ITEM_TILES + FINISH_LAG):
            if step < ITEM_TILES:
                first_product(step)
            if 0 <= step - QUANTISE_LAG < ITEM_TILES:
                quantise(n_grouped, n_codes, n_scales, (step - QUANTISE_LAG) * P, P)
            if 0 <= step - SECOND_LAG < ITEM_TILES:
                biased.append(second_product(step - SECOND_LAG))
            if 0 <= step - FINISH_LAG:
                finish(step - FINISH_LAG, biased[step - FINISH_LAG])
